import numpy as np
import ml_dtypes

BF16 = ml_dtypes.bfloat16


def bf(x):
    return np.asarray(x, np.float32).astype(BF16)


def f32(x):
    return np.asarray(x, np.float32)


def f64(x):
    return np.asarray(x).astype(np.float64)


def striped(idx):
    return np.tile(idx.reshape(-1, 16).T, (8, 1))


D, S, F, N = 128, 512, 4, 2048


def setup_inputs():
    return {"table": bf(np.random.standard_normal((D, S))), "w": bf(np.random.standard_normal((D, D)) / np.sqrt(D)), "b1": f32(0.3 * np.random.standard_normal((D, 1))), "w2": bf(np.random.standard_normal((D, 1)) / np.sqrt(D)), "b2": f32(0.5 + 0.1 * np.random.standard_normal((1, 1))), "offs": striped(np.concatenate([np.random.permutation(S) for _ in range(F)]))}


def reference(table, w, b1, w2, b2, offs):
    idx = offs[:16].T.reshape(-1)
    h = np.tanh(f64(w).T @ f64(table)[:, idx] + f64(b1))
    pool = h.reshape(D, S, F).max(axis=2)
    return f64(w2).T @ pool + f64(b2)

@@ -1,0 +1,64 @@
+import concourse.mybir as mybir
+
+BF16, F32, U16 = mybir.dt.bfloat16, mybir.dt.float32, mybir.dt.uint16
+
+D = 128
+S = 512
+F = 4
+N = S * F
+PIECE = 512
+WORDS = PIECE // F
+PER_COLUMN = 16
+
+FLOPS = 2 * D * D * N + 2 * D * S
+
+
+def tile_wordweightinglayer_kernel(tc, table, w, b1, w2, b2, offs, out):
+    nc = tc.nc
+    with (
+        tc.tile_pool(name="held", bufs=1) as held,
+        tc.tile_pool(name="work", bufs=2) as work,
+        tc.psum_pool(name="banks", bufs=2) as banks,
+        tc.psum_pool(name="last", bufs=1) as last,
+    ):
+        offsets = held.tile([D, N // PER_COLUMN], U16, name="offsets")
+        nc.sync.dma_start(offsets[:], offs)
+        table_sb = held.tile([D, S], BF16, name="table_sb")
+        nc.scalar.dma_start(table_sb[:], table)
+        w_sb = held.tile([D, D], BF16, name="w_sb")
+        nc.sync.dma_start(w_sb[:], w)
+        b1_sb = held.tile([D, 1], F32, name="b1_sb")
+        nc.gpsimd.dma_start(b1_sb[:], b1)
+        w2_sb = held.tile([D, 1], BF16, name="w2_sb")
+        nc.gpsimd.dma_start(w2_sb[:], w2)
+        b2_sb = held.tile([1, 1], F32, name="b2_sb")
+        nc.gpsimd.dma_start(b2_sb[:], b2)
+
+        pooled = held.tile([D, S], BF16, name="pooled")
+        for k in range(N // PIECE):
+            columns = PIECE // PER_COLUMN
+            projected = banks.tile([D, PIECE], F32, name="projected")
+            nc.tensor.matmul(
+                projected[:],
+                w_sb[:],
+                table_sb[:].indirect(offsets[:, k * columns : (k + 1) * columns]),
+                start=True,
+                stop=True,
+            )
+            h = work.tile([D, PIECE], F32, name="h")
+            nc.scalar.activation(
+                h[:], projected[:], mybir.ActivationFunctionType.Tanh, bias=b1_sb[:]
+            )
+            with nc.allow_low_precision(reason="a maximum adds nothing up"):
+                nc.vector.tensor_reduce(
+                    pooled[:, k * WORDS : (k + 1) * WORDS],
+                    h[:].rearrange("m (t f) -> m t f", f=F),
+                    mybir.AxisListType.X,
+                    mybir.AluOpType.max,
+                )
+
+        score = last.tile([1, S], F32, name="score")
+        nc.tensor.matmul(score[:], w2_sb[:], pooled[:], start=True, stop=True)
+        out_sb = held.tile([1, S], F32, name="out_sb")
+        nc.vector.tensor_scalar_add(out_sb[:], score[:], b2_sb[:])
+        nc.sync.dma_start(out, out_sb[:])

@@ -28,11 +28,17 @@ def tile_wordweightinglayer_kernel(tc, table, w, b1, w2, b2, offs, out):
         w_sb = held.tile([D, D], BF16, name="w_sb")
         nc.sync.dma_start(w_sb[:], w)
         b1_sb = held.tile([D, 1], F32, name="b1_sb")
-        nc.gpsimd.dma_start(b1_sb[:], b1)
+        nc.scalar.dma_start(b1_sb[:], b1)
         w2_sb = held.tile([D, 1], BF16, name="w2_sb")
-        nc.gpsimd.dma_start(w2_sb[:], w2)
+        nc.sync.dma_start(w2_sb[:], w2)
         b2_sb = held.tile([1, 1], F32, name="b2_sb")
-        nc.gpsimd.dma_start(b2_sb[:], b2)
+        nc.scalar.dma_start(b2_sb[:], b2)
+
+        scratch = held.tile([D, 1], F32, name="scratch")
+        nc.vector.memset(scratch[:], 0.0)
+        nc.scalar.activation(
+            scratch[:], scratch[:], mybir.ActivationFunctionType.Tanh
+        )
 
         pooled = held.tile([D, S], BF16, name="pooled")
         for k in range(N // PIECE):

@@ -51,17 +51,19 @@ def tile_wordweightinglayer_kernel(tc, table, w, b1, w2, b2, offs, out):
                 start=True,
                 stop=True,
             )
-            h = work.tile([D, PIECE], F32, name="h")
-            nc.scalar.activation(
-                h[:], projected[:], mybir.ActivationFunctionType.Tanh, bias=b1_sb[:]
+            largest = work.tile([D, WORDS], F32, name="largest")
+            nc.vector.tensor_reduce(
+                largest[:],
+                projected[:].rearrange("m (t f) -> m t f", f=F),
+                mybir.AxisListType.X,
+                mybir.AluOpType.max,
             )
-            with nc.allow_low_precision(reason="a maximum adds nothing up"):
-                nc.vector.tensor_reduce(
-                    pooled[:, k * WORDS : (k + 1) * WORDS],
-                    h[:].rearrange("m (t f) -> m t f", f=F),
-                    mybir.AxisListType.X,
-                    mybir.AluOpType.max,
-                )
+            nc.scalar.activation(
+                pooled[:, k * WORDS : (k + 1) * WORDS],
+                largest[:],
+                mybir.ActivationFunctionType.Tanh,
+                bias=b1_sb[:],
+            )
 
         score = last.tile([1, S], F32, name="score")
         nc.tensor.matmul(score[:], w2_sb[:], pooled[:], start=True, stop=True)

@@ -9,6 +9,7 @@ N = S * F
 PIECE = 512
 WORDS = PIECE // F
 PER_COLUMN = 16
+WARM_UP = 6
 
 FLOPS = 2 * D * D * N + 2 * D * S
 
@@ -39,6 +40,12 @@ def tile_wordweightinglayer_kernel(tc, table, w, b1, w2, b2, offs, out):
         nc.scalar.activation(
             scratch[:], scratch[:], mybir.ActivationFunctionType.Tanh
         )
+
+        zeros = held.tile([D, PIECE], BF16, name="zeros")
+        nc.vector.memset(zeros[:], 0.0)
+        unread = last.tile([D, PIECE], F32, name="unread")
+        for i in range(WARM_UP):
+            nc.tensor.matmul(unread[:], zeros[:, 0:D], zeros[:], start=True, stop=True)
 
         pooled = held.tile([D, S], BF16, name="pooled")
         for k in range(N // PIECE):

@@ -7,9 +7,9 @@ S = 512
 F = 4
 N = S * F
 PIECE = 512
+PIECES = N // PIECE
 WORDS = PIECE // F
 PER_COLUMN = 16
-WARM_UP = 6
 
 FLOPS = 2 * D * D * N + 2 * D * S
 
@@ -19,8 +19,8 @@ def tile_wordweightinglayer_kernel(tc, table, w, b1, w2, b2, offs, out):
     with (
         tc.tile_pool(name="held", bufs=1) as held,
         tc.tile_pool(name="work", bufs=2) as work,
-        tc.psum_pool(name="banks", bufs=2) as banks,
-        tc.psum_pool(name="last", bufs=1) as last,
+        tc.psum_pool(name="banks", bufs=PIECES) as banks,
+        tc.psum_pool(name="rows", bufs=PIECES) as rows,
     ):
         offsets = held.tile([D, N // PER_COLUMN], U16, name="offsets")
         nc.sync.dma_start(offsets[:], offs)
@@ -41,14 +41,8 @@ def tile_wordweightinglayer_kernel(tc, table, w, b1, w2, b2, offs, out):
             scratch[:], scratch[:], mybir.ActivationFunctionType.Tanh
         )
 
-        zeros = held.tile([D, PIECE], BF16, name="zeros")
-        nc.vector.memset(zeros[:], 0.0)
-        unread = last.tile([D, PIECE], F32, name="unread")
-        for i in range(WARM_UP):
-            nc.tensor.matmul(unread[:], zeros[:, 0:D], zeros[:], start=True, stop=True)
-
         pooled = held.tile([D, S], BF16, name="pooled")
-        for k in range(N // PIECE):
+        for k in range(PIECES):
             columns = PIECE // PER_COLUMN
             projected = banks.tile([D, PIECE], F32, name="projected")
             nc.tensor.matmul(
@@ -72,8 +66,15 @@ def tile_wordweightinglayer_kernel(tc, table, w, b1, w2, b2, offs, out):
                 bias=b1_sb[:],
             )
 
-        score = last.tile([1, S], F32, name="score")
-        nc.tensor.matmul(score[:], w2_sb[:], pooled[:], start=True, stop=True)
         out_sb = held.tile([1, S], F32, name="out_sb")
-        nc.vector.tensor_scalar_add(out_sb[:], score[:], b2_sb[:])
+        for k in range(PIECES):
+            words = slice(k * WORDS, (k + 1) * WORDS)
+            score = rows.tile([1, WORDS], F32, name="score")
+            nc.tensor.matmul(score[:], w2_sb[:], pooled[:, words], start=True, stop=True)
+            nc.scalar.activation(
+                out_sb[:, words],
+                score[:],
+                mybir.ActivationFunctionType.Identity,
+                bias=b2_sb[:],
+            )
         nc.sync.dma_start(out, out_sb[:])

@@ -10,6 +10,7 @@ PIECE = 512
 PIECES = N // PIECE
 WORDS = PIECE // F
 PER_COLUMN = 16
+WARM_UP = 16
 
 FLOPS = 2 * D * D * N + 2 * D * S
 
@@ -20,7 +21,8 @@ def tile_wordweightinglayer_kernel(tc, table, w, b1, w2, b2, offs, out):
         tc.tile_pool(name="held", bufs=1) as held,
         tc.tile_pool(name="work", bufs=2) as work,
         tc.psum_pool(name="banks", bufs=PIECES) as banks,
-        tc.psum_pool(name="rows", bufs=PIECES) as rows,
+        tc.psum_pool(name="rows", bufs=PIECES - 1) as rows,
+        tc.psum_pool(name="spare", bufs=1) as spare,
     ):
         offsets = held.tile([D, N // PER_COLUMN], U16, name="offsets")
         nc.sync.dma_start(offsets[:], offs)
@@ -34,6 +36,12 @@ def tile_wordweightinglayer_kernel(tc, table, w, b1, w2, b2, offs, out):
         nc.sync.dma_start(w2_sb[:], w2)
         b2_sb = held.tile([1, 1], F32, name="b2_sb")
         nc.scalar.dma_start(b2_sb[:], b2)
+
+        zeros = held.tile([D, D], BF16, name="zeros")
+        nc.vector.memset(zeros[:], 0.0)
+        unread = spare.tile([D, D], F32, name="unread")
+        for i in range(WARM_UP):
+            nc.tensor.matmul(unread[:], zeros[:], zeros[:], start=True, stop=True)
 
         scratch = held.tile([D, 1], F32, name="scratch")
         nc.vector.memset(scratch[:], 0.0)

@@ -7,10 +7,11 @@ S = 512
 F = 4
 N = S * F
 PIECE = 512
-PIECES = N // PIECE
-WORDS = PIECE // F
 PER_COLUMN = 16
-WARM_UP = 16
+
+SIZES = [PIECE // 2] + [PIECE] * (N // PIECE - 1) + [PIECE // 2]
+STARTS = [sum(SIZES[:k]) for k in range(len(SIZES))]
+BANKS = 4
 
 FLOPS = 2 * D * D * N + 2 * D * S
 
@@ -20,9 +21,8 @@ def tile_wordweightinglayer_kernel(tc, table, w, b1, w2, b2, offs, out):
     with (
         tc.tile_pool(name="held", bufs=1) as held,
         tc.tile_pool(name="work", bufs=2) as work,
-        tc.psum_pool(name="banks", bufs=PIECES) as banks,
-        tc.psum_pool(name="rows", bufs=PIECES - 1) as rows,
-        tc.psum_pool(name="spare", bufs=1) as spare,
+        tc.psum_pool(name="banks", bufs=BANKS) as banks,
+        tc.psum_pool(name="rows", bufs=BANKS) as rows,
     ):
         offsets = held.tile([D, N // PER_COLUMN], U16, name="offsets")
         nc.sync.dma_start(offsets[:], offs)
@@ -37,12 +37,6 @@ def tile_wordweightinglayer_kernel(tc, table, w, b1, w2, b2, offs, out):
         b2_sb = held.tile([1, 1], F32, name="b2_sb")
         nc.scalar.dma_start(b2_sb[:], b2)
 
-        zeros = held.tile([D, D], BF16, name="zeros")
-        nc.vector.memset(zeros[:], 0.0)
-        unread = spare.tile([D, D], F32, name="unread")
-        for i in range(WARM_UP):
-            nc.tensor.matmul(unread[:], zeros[:], zeros[:], start=True, stop=True)
-
         scratch = held.tile([D, 1], F32, name="scratch")
         nc.vector.memset(scratch[:], 0.0)
         nc.scalar.activation(
@@ -50,38 +44,41 @@ def tile_wordweightinglayer_kernel(tc, table, w, b1, w2, b2, offs, out):
         )
 
         pooled = held.tile([D, S], BF16, name="pooled")
-        for k in range(PIECES):
-            columns = PIECE // PER_COLUMN
+        for start, size in zip(STARTS, SIZES):
             projected = banks.tile([D, PIECE], F32, name="projected")
             nc.tensor.matmul(
-                projected[:],
+                projected[:, 0:size],
                 w_sb[:],
-                table_sb[:].indirect(offsets[:, k * columns : (k + 1) * columns]),
+                table_sb[:].indirect(
+                    offsets[:, start // PER_COLUMN : (start + size) // PER_COLUMN]
+                ),
                 start=True,
                 stop=True,
             )
-            largest = work.tile([D, WORDS], F32, name="largest")
+            largest = work.tile([D, PIECE // F], F32, name="largest")
             nc.vector.tensor_reduce(
-                largest[:],
-                projected[:].rearrange("m (t f) -> m t f", f=F),
+                largest[:, 0 : size // F],
+                projected[:, 0:size].rearrange("m (t f) -> m t f", f=F),
                 mybir.AxisListType.X,
                 mybir.AluOpType.max,
             )
             nc.scalar.activation(
-                pooled[:, k * WORDS : (k + 1) * WORDS],
-                largest[:],
+                pooled[:, start // F : (start + size) // F],
+                largest[:, 0 : size // F],
                 mybir.ActivationFunctionType.Tanh,
                 bias=b1_sb[:],
             )
 
         out_sb = held.tile([1, S], F32, name="out_sb")
-        for k in range(PIECES):
-            words = slice(k * WORDS, (k + 1) * WORDS)
-            score = rows.tile([1, WORDS], F32, name="score")
-            nc.tensor.matmul(score[:], w2_sb[:], pooled[:, words], start=True, stop=True)
+        for start, size in zip(STARTS, SIZES):
+            words = slice(start // F, (start + size) // F)
+            score = rows.tile([1, PIECE // F], F32, name="score")
+            nc.tensor.matmul(
+                score[:, 0 : size // F], w2_sb[:], pooled[:, words], start=True, stop=True
+            )
             nc.scalar.activation(
                 out_sb[:, words],
-                score[:],
+                score[:, 0 : size // F],
                 mybir.ActivationFunctionType.Identity,
                 bias=b2_sb[:],
             )

@@ -7,11 +7,9 @@ S = 512
 F = 4
 N = S * F
 PIECE = 512
+PIECES = N // PIECE
+WORDS = PIECE // F
 PER_COLUMN = 16
-
-SIZES = [PIECE // 2] + [PIECE] * (N // PIECE - 1) + [PIECE // 2]
-STARTS = [sum(SIZES[:k]) for k in range(len(SIZES))]
-BANKS = 4
 
 FLOPS = 2 * D * D * N + 2 * D * S
 
@@ -21,8 +19,8 @@ def tile_wordweightinglayer_kernel(tc, table, w, b1, w2, b2, offs, out):
     with (
         tc.tile_pool(name="held", bufs=1) as held,
         tc.tile_pool(name="work", bufs=2) as work,
-        tc.psum_pool(name="banks", bufs=BANKS) as banks,
-        tc.psum_pool(name="rows", bufs=BANKS) as rows,
+        tc.psum_pool(name="banks", bufs=PIECES) as banks,
+        tc.psum_pool(name="rows", bufs=PIECES) as rows,
     ):
         offsets = held.tile([D, N // PER_COLUMN], U16, name="offsets")
         nc.sync.dma_start(offsets[:], offs)
@@ -44,42 +42,39 @@ def tile_wordweightinglayer_kernel(tc, table, w, b1, w2, b2, offs, out):
         )
 
         pooled = held.tile([D, S], BF16, name="pooled")
-        for start, size in zip(STARTS, SIZES):
+        for k in range(PIECES):
+            columns = PIECE // PER_COLUMN
             projected = banks.tile([D, PIECE], F32, name="projected")
             nc.tensor.matmul(
-                projected[:, 0:size],
+                projected[:],
                 w_sb[:],
-                table_sb[:].indirect(
-                    offsets[:, start // PER_COLUMN : (start + size) // PER_COLUMN]
-                ),
+                table_sb[:].indirect(offsets[:, k * columns : (k + 1) * columns]),
                 start=True,
                 stop=True,
             )
-            largest = work.tile([D, PIECE // F], F32, name="largest")
+            largest = work.tile([D, WORDS], F32, name="largest")
             nc.vector.tensor_reduce(
-                largest[:, 0 : size // F],
-                projected[:, 0:size].rearrange("m (t f) -> m t f", f=F),
+                largest[:],
+                projected[:].rearrange("m (t f) -> m t f", f=F),
                 mybir.AxisListType.X,
                 mybir.AluOpType.max,
             )
             nc.scalar.activation(
-                pooled[:, start // F : (start + size) // F],
-                largest[:, 0 : size // F],
+                pooled[:, k * WORDS : (k + 1) * WORDS],
+                largest[:],
                 mybir.ActivationFunctionType.Tanh,
                 bias=b1_sb[:],
             )
 
         out_sb = held.tile([1, S], F32, name="out_sb")
-        for start, size in zip(STARTS, SIZES):
-            words = slice(start // F, (start + size) // F)
-            score = rows.tile([1, PIECE // F], F32, name="score")
-            nc.tensor.matmul(
-                score[:, 0 : size // F], w2_sb[:], pooled[:, words], start=True, stop=True
-            )
+        for k in range(PIECES):
+            words = slice(k * WORDS, (k + 1) * WORDS)
+            score = rows.tile([1, WORDS], F32, name="score")
+            nc.tensor.matmul(score[:], w2_sb[:], pooled[:, words], start=True, stop=True)
             nc.scalar.activation(
                 out_sb[:, words],
-                score[:, 0 : size // F],
+                score[:],
                 mybir.ActivationFunctionType.Identity,
                 bias=b2_sb[:],
             )
-        nc.sync.dma_start(out, out_sb[:])
+        nc.scalar.dma_start(out, out_sb[:])

@@ -18,7 +18,7 @@ def tile_wordweightinglayer_kernel(tc, table, w, b1, w2, b2, offs, out):
     nc = tc.nc
     with (
         tc.tile_pool(name="held", bufs=1) as held,
-        tc.tile_pool(name="work", bufs=2) as work,
+        tc.tile_pool(name="work", bufs=PIECES) as work,
         tc.psum_pool(name="banks", bufs=PIECES) as banks,
         tc.psum_pool(name="rows", bufs=PIECES) as rows,
     ):

@@ -6,10 +6,10 @@ D = 128
 S = 512
 F = 4
 N = S * F
-PIECE = 512
-PIECES = N // PIECE
-WORDS = PIECE // F
+BANK = 512
 PER_COLUMN = 16
+PIECES = (512, 512, 512, 256, 256)
+assert sum(PIECES) == N
 
 FLOPS = 2 * D * D * N + 2 * D * S
 
@@ -18,9 +18,9 @@ def tile_wordweightinglayer_kernel(tc, table, w, b1, w2, b2, offs, out):
     nc = tc.nc
     with (
         tc.tile_pool(name="held", bufs=1) as held,
-        tc.tile_pool(name="work", bufs=PIECES) as work,
-        tc.psum_pool(name="banks", bufs=PIECES) as banks,
-        tc.psum_pool(name="rows", bufs=PIECES) as rows,
+        tc.tile_pool(name="work", bufs=len(PIECES)) as work,
+        tc.psum_pool(name="banks", bufs=5) as banks,
+        tc.psum_pool(name="rows", bufs=3) as rows,
     ):
         offsets = held.tile([D, N // PER_COLUMN], U16, name="offsets")
         nc.sync.dma_start(offsets[:], offs)
@@ -42,39 +42,46 @@ def tile_wordweightinglayer_kernel(tc, table, w, b1, w2, b2, offs, out):
         )
 
         pooled = held.tile([D, S], BF16, name="pooled")
-        for k in range(PIECES):
-            columns = PIECE // PER_COLUMN
-            projected = banks.tile([D, PIECE], F32, name="projected")
+        first = 0
+        for entries in PIECES:
+            projected = banks.tile([D, BANK], F32, name="projected")
             nc.tensor.matmul(
-                projected[:],
+                projected[:, :entries],
                 w_sb[:],
-                table_sb[:].indirect(offsets[:, k * columns : (k + 1) * columns]),
+                table_sb[:].indirect(
+                    offsets[:, first // PER_COLUMN : (first + entries) // PER_COLUMN]
+                ),
                 start=True,
                 stop=True,
             )
-            largest = work.tile([D, WORDS], F32, name="largest")
+            largest = work.tile([D, entries // F], F32, name="largest")
             nc.vector.tensor_reduce(
                 largest[:],
-                projected[:].rearrange("m (t f) -> m t f", f=F),
+                projected[:, :entries].rearrange("m (t f) -> m t f", f=F),
                 mybir.AxisListType.X,
                 mybir.AluOpType.max,
             )
             nc.scalar.activation(
-                pooled[:, k * WORDS : (k + 1) * WORDS],
+                pooled[:, first // F : (first + entries) // F],
                 largest[:],
                 mybir.ActivationFunctionType.Tanh,
                 bias=b1_sb[:],
             )
+            first += entries
 
         out_sb = held.tile([1, S], F32, name="out_sb")
-        for k in range(PIECES):
-            words = slice(k * WORDS, (k + 1) * WORDS)
-            score = rows.tile([1, WORDS], F32, name="score")
-            nc.tensor.matmul(score[:], w2_sb[:], pooled[:, words], start=True, stop=True)
+        first = 0
+        for entries in PIECES:
+            words = slice(first // F, (first + entries) // F)
+            score = rows.tile([1, BANK], F32, name="score")
+            nc.tensor.matmul(
+                score[:, : entries // F], w2_sb[:], pooled[:, words], start=True, stop=True
+            )
             nc.scalar.activation(
                 out_sb[:, words],
-                score[:],
+                score[:, : entries // F],
                 mybir.ActivationFunctionType.Identity,
                 bias=b2_sb[:],
             )
+            first += entries
         nc.scalar.dma_start(out, out_sb[:])

@@ -22,12 +22,12 @@ def tile_wordweightinglayer_kernel(tc, table, w, b1, w2, b2, offs, out):
         tc.psum_pool(name="banks", bufs=5) as banks,
         tc.psum_pool(name="rows", bufs=3) as rows,
     ):
+        table_sb = held.tile([D, S], BF16, name="table_sb")
+        nc.sync.dma_start(table_sb[:], table)
+        w_sb = held.tile([D, D], BF16, name="w_sb")
+        nc.scalar.dma_start(w_sb[:], w)
         offsets = held.tile([D, N // PER_COLUMN], U16, name="offsets")
         nc.sync.dma_start(offsets[:], offs)
-        table_sb = held.tile([D, S], BF16, name="table_sb")
-        nc.scalar.dma_start(table_sb[:], table)
-        w_sb = held.tile([D, D], BF16, name="w_sb")
-        nc.sync.dma_start(w_sb[:], w)
         b1_sb = held.tile([D, 1], F32, name="b1_sb")
         nc.scalar.dma_start(b1_sb[:], b1)
         w2_sb = held.tile([D, 1], BF16, name="w2_sb")

@@ -7,6 +7,8 @@ S = 512
 F = 4
 N = S * F
 BANK = 512
+RUNS = 4
+GAP = 8
 PER_COLUMN = 16
 PIECES = (512, 512, 512, 256, 256)
 assert sum(PIECES) == N
@@ -69,19 +71,22 @@ def tile_wordweightinglayer_kernel(tc, table, w, b1, w2, b2, offs, out):
             )
             first += entries
 
-        out_sb = held.tile([1, S], F32, name="out_sb")
+        out_sb = held.tile([1, RUNS, S // RUNS + GAP], F32, name="out_sb")
         first = 0
         for entries in PIECES:
             words = slice(first // F, (first + entries) // F)
+            run, column = divmod(first // F, S // RUNS)
             score = rows.tile([1, BANK], F32, name="score")
             nc.tensor.matmul(
                 score[:, : entries // F], w2_sb[:], pooled[:, words], start=True, stop=True
             )
             nc.scalar.activation(
-                out_sb[:, words],
+                out_sb[:, run, column : column + entries // F],
                 score[:, : entries // F],
                 mybir.ActivationFunctionType.Identity,
                 bias=b2_sb[:],
             )
             first += entries
-        nc.scalar.dma_start(out, out_sb[:])
+        nc.scalar.dma_start(
+            out.rearrange("o (r c) -> o r c", r=RUNS), out_sb[:, :, : S // RUNS]
+        )

@@ -7,7 +7,7 @@ S = 512
 F = 4
 N = S * F
 BANK = 512
-RUNS = 4
+RUNS = 2
 GAP = 8
 PER_COLUMN = 16
 PIECES = (512, 512, 512, 256, 256)

@@ -10,7 +10,7 @@ BANK = 512
 RUNS = 2
 GAP = 8
 PER_COLUMN = 16
-PIECES = (512, 512, 512, 256, 256)
+PIECES = (512, 512, 512, 320, 192)
 assert sum(PIECES) == N
 
 FLOPS = 2 * D * D * N + 2 * D * S
@@ -80,11 +80,10 @@ def tile_wordweightinglayer_kernel(tc, table, w, b1, w2, b2, offs, out):
             nc.tensor.matmul(
                 score[:, : entries // F], w2_sb[:], pooled[:, words], start=True, stop=True
             )
-            nc.scalar.activation(
+            nc.vector.tensor_scalar_add(
                 out_sb[:, run, column : column + entries // F],
                 score[:, : entries // F],
-                mybir.ActivationFunctionType.Identity,
-                bias=b2_sb[:],
+                b2_sb[:],
             )
             first += entries
         nc.scalar.dma_start(

import concourse.mybir as mybir

BF16, F32, U16 = mybir.dt.bfloat16, mybir.dt.float32, mybir.dt.uint16

D = 128
S = 512
F = 4
N = S * F
BANK = 512
RUNS = 2
GAP = 8
PER_COLUMN = 16
PIECES = (512, 512, 512, 320, 192)
assert sum(PIECES) == N

FLOPS = 2 * D * D * N + 2 * D * S


def tile_wordweightinglayer_kernel(tc, table, w, b1, w2, b2, offs, out):
    nc = tc.nc
    with (
        tc.tile_pool(name="held", bufs=1) as held,
        tc.tile_pool(name="work", bufs=len(PIECES)) as work,
        tc.psum_pool(name="banks", bufs=5) as banks,
        tc.psum_pool(name="rows", bufs=3) as rows,
    ):
        table_sb = held.tile([D, S], BF16, name="table_sb")
        nc.sync.dma_start(table_sb[:], table)
        w_sb = held.tile([D, D], BF16, name="w_sb")
        nc.scalar.dma_start(w_sb[:], w)
        offsets = held.tile([D, N // PER_COLUMN], U16, name="offsets")
        nc.sync.dma_start(offsets[:], offs)
        b1_sb = held.tile([D, 1], F32, name="b1_sb")
        nc.scalar.dma_start(b1_sb[:], b1)
        w2_sb = held.tile([D, 1], BF16, name="w2_sb")
        nc.sync.dma_start(w2_sb[:], w2)
        b2_sb = held.tile([1, 1], F32, name="b2_sb")
        nc.scalar.dma_start(b2_sb[:], b2)

        scratch = held.tile([D, 1], F32, name="scratch")
        nc.vector.memset(scratch[:], 0.0)
        nc.scalar.activation(
            scratch[:], scratch[:], mybir.ActivationFunctionType.Tanh
        )

        pooled = held.tile([D, S], BF16, name="pooled")
        first = 0
        for entries in PIECES:
            projected = banks.tile([D, BANK], F32, name="projected")
            nc.tensor.matmul(
                projected[:, :entries],
                w_sb[:],
                table_sb[:].indirect(
                    offsets[:, first // PER_COLUMN : (first + entries) // PER_COLUMN]
                ),
                start=True,
                stop=True,
            )
            largest = work.tile([D, entries // F], F32, name="largest")
            nc.vector.tensor_reduce(
                largest[:],
                projected[:, :entries].rearrange("m (t f) -> m t f", f=F),
                mybir.AxisListType.X,
                mybir.AluOpType.max,
            )
            nc.scalar.activation(
                pooled[:, first // F : (first + entries) // F],
                largest[:],
                mybir.ActivationFunctionType.Tanh,
                bias=b1_sb[:],
            )
            first += entries

        out_sb = held.tile([1, RUNS, S // RUNS + GAP], F32, name="out_sb")
        first = 0
        for entries in PIECES:
            words = slice(first // F, (first + entries) // F)
            run, column = divmod(first // F, S // RUNS)
            score = rows.tile([1, BANK], F32, name="score")
            nc.tensor.matmul(
                score[:, : entries // F], w2_sb[:], pooled[:, words], start=True, stop=True
            )
            nc.vector.tensor_scalar_add(
                out_sb[:, run, column : column + entries // F],
                score[:, : entries // F],
                b2_sb[:],
            )
            first += entries
        nc.scalar.dma_start(
            out.rearrange("o (r c) -> o r c", r=RUNS), out_sb[:, :, : S // RUNS]
        )
